import numpy as np
import ml_dtypes


def mxq(x, axis, fmt="e4m3"):
    dtype, down = {"e4m3": (ml_dtypes.float8_e4m3fn, 7), "e5m2": (ml_dtypes.float8_e5m2, 14)}[fmt]
    v = np.moveaxis(np.asarray(x, np.float32).astype(ml_dtypes.bfloat16).astype(np.float64), axis, -1)
    blocks = v.reshape(v.shape[:-1] + (-1, 32))
    amax = np.abs(blocks).max(-1, keepdims=True)
    byte = np.maximum(np.where(amax > 0, np.frexp(amax)[1] - 1 + 127, 0) - down, 1)
    scale = np.exp2(byte - 127.0)
    codes = (blocks / scale).astype(np.float32).astype(dtype).astype(np.float64)
    return np.moveaxis((codes * scale).reshape(v.shape), -1, axis)


WIDE = False


def mx_kscale(k):
    if not WIDE:
        return np.ones(k)
    levels = np.array([10, -10, 5, -5, 0])
    a = np.random.permutation(np.resize(levels, k // 512 * 4)).reshape(k // 512, 4)
    idx = np.arange(k)
    return np.exp2(a[idx // 512, idx % 128 // 32])


BF16 = ml_dtypes.bfloat16


def bf(x):
    return np.asarray(x, np.float32).astype(BF16)


def f64(x):
    return np.asarray(x).astype(np.float64)


B, N, DIN, H, EMB, CHEB = 2, 512, 128, 128, 10, 2
C = DIN + H
KC = CHEB * C
G = 2 * H


def sigmoid(v):
    return 1.0 / (1.0 + np.exp(-v))


def draw_supports():
    emb = f64(bf(np.random.standard_normal((N, EMB))))
    l = np.maximum((emb[:, None, :] * emb[None, :, :]).sum(-1), 0.0)
    e = np.exp(l - l.max(1, keepdims=True))
    return e / e.sum(1, keepdims=True)


def setup_inputs():
    s = mx_kscale(KC)
    return {"xg": bf(np.random.standard_normal((B, N, KC)) * 0.8 * s),
            "W_gate": bf(np.random.standard_normal((KC, G)) * np.sqrt(2.0 / (KC + G)) / s[:, None]),
            "b_gate": bf(np.random.standard_normal(G) * 0.3),
            "x": bf(np.random.standard_normal((B, N, DIN))),
            "state": bf(np.random.standard_normal((B, N, H))),
            "supports": bf(draw_supports())}


def reference(xg, W_gate, b_gate, x, state, supports):
    z_r = sigmoid((mxq(f64(xg), 2, "e4m3") @ mxq(f64(W_gate), 0, "e4m3")) + f64(b_gate))
    z, r = z_r[..., :H], z_r[..., H:]
    cand = np.concatenate([f64(x), z * f64(state)], -1)
    c1 = mxq(f64(supports), 1, "e4m3") @ mxq(cand, 1, "e4m3")
    return r, cand, c1

@@ -1,0 +1,239 @@
+import concourse.mybir as mybir
+from concourse.masks import make_identity
+
+BF16 = mybir.dt.bfloat16
+F32 = mybir.dt.float32
+U32 = mybir.dt.uint32
+U8 = mybir.dt.uint8
+FP8X4 = mybir.dt.float8_e4m3fn_x4
+ADD = mybir.AluOpType.add
+MULT = mybir.AluOpType.mult
+SIGMOID = mybir.ActivationFunctionType.Sigmoid
+
+P = 128
+PACK = 4
+B = 2
+N = 512
+H = 128
+G = 2 * H
+BLOCKS = N // P
+
+FLOPS = 2 * B * N * N * G + 2 * B * N * N * G
+
+
+def tile_agcrncell_pb_s_kernel(
+    tc, xg, W_gate, b_gate, x, state, supports, out_0, out_1, out_2
+):
+    nc = tc.nc
+    with tc.tile_pool(name="keep", bufs=1) as keep, tc.psum_pool(name="psum", bufs=8) as psum:
+        xg_sb = keep.tile([P, B * 2, 2, N], BF16)
+        w_sb = keep.tile([P, PACK, G], BF16)
+        s_sb = keep.tile([P, BLOCKS, N], BF16)
+        x_sb = keep.tile([P, B * BLOCKS, H], BF16)
+        state_sb = keep.tile([P, B * BLOCKS, H], BF16)
+        bias_row = keep.tile([P, G], BF16)
+
+        nc.vector.memset(bias_row[:], 0.0)
+        nc.scalar.dma_start(out=bias_row[0:1, :], in_=b_gate.unsqueeze(0))
+
+        def load_xg(b, u):
+            nc.sync.dma_start(
+                out=xg_sb[:, 2 * b + u],
+                in_=xg[b].rearrange("(u p e) k -> u p e k", u=2, e=2)[u],
+            )
+
+        load_xg(0, 0)
+        load_xg(0, 1)
+        nc.sync.dma_start(
+            out=w_sb[:].rearrange("p (u e) c -> p u e c", u=2),
+            in_=W_gate.rearrange("(u p e) c -> p u e c", u=2, e=2),
+        )
+        load_xg(1, 0)
+        load_xg(1, 1)
+        nc.sync.dma_start(out=s_sb[:], in_=supports.rearrange("(p j) m -> p j m", j=BLOCKS))
+        nc.sync.dma_start(
+            out=x_sb[:].rearrange("p (h e) c -> p h (e c)", e=2),
+            in_=x.rearrange("b (u p e) c -> p (b u) (e c)", u=2, e=2),
+        )
+        nc.sync.dma_start(
+            out=state_sb[:].rearrange("p (h e) c -> p h (e c)", e=2),
+            in_=state.rearrange("b (u p e) c -> p (b u) (e c)", u=2, e=2),
+        )
+
+        ident = keep.tile([P, P], F32)
+        make_identity(nc, ident[:])
+        ones = keep.tile([P, P], BF16)
+        nc.vector.memset(ones[:], 1.0)
+        warm_in = keep.tile([P, 1], F32)
+        warm_out = keep.tile([P, 1], F32)
+        nc.vector.memset(warm_in[:], 0.0)
+        nc.scalar.activation(out=warm_out[:], in_=warm_in[:], func=SIGMOID)
+
+        bias_ps = psum.tile([P, G], F32, tag="bank")
+        nc.tensor.matmul(out=bias_ps[:], lhsT=ones[:], rhs=bias_row[:], start=True, stop=True)
+        bias_all = keep.tile([P, G], F32)
+        nc.scalar.copy(out=bias_all[:], in_=bias_ps[:])
+
+        w_grouped = keep.tile([P, G, PACK], BF16, align_bytes=64)
+        w_codes = keep.tile([P, G], U32, align_bytes=64)
+        w_scales = keep.tile([P, G], U8, align_bytes=64)
+        nc.vector.tensor_copy(out=w_grouped[:], in_=w_sb[:].rearrange("p t c -> p c t"))
+        nc.vector.quantize_mx(
+            out=w_codes[:].bitcast(FP8X4),
+            scales=w_scales[:],
+            in_=w_grouped[:].rearrange("p c t -> p (c t)"),
+        )
+
+        def quantise_rows(rows, grouped, codes, scales):
+            bank = psum.tile([P, 2, 2, P], F32, tag="bank")
+            for i in range(2):
+                words = rows[:, i, :].bitcast(F32)
+                for u in range(2):
+                    nc.tensor.transpose(bank[:, i, u, :], words[:, P * u : P * (u + 1)], ident[:])
+            nc.scalar.copy(
+                out=grouped.bitcast(F32), in_=bank[:].rearrange("p i u r -> p i r u")
+            )
+            nc.vector.quantize_mx(
+                out=codes.bitcast(FP8X4),
+                scales=scales,
+                in_=grouped.rearrange("p i r t -> p (i r t)"),
+            )
+
+        xg_grouped = keep.tile([P, B * 2, 2, P, PACK], BF16, align_bytes=64)
+        xg_codes = keep.tile([P, B * N], U32, align_bytes=64)
+        xg_scales = keep.tile([P, B * N], U8, align_bytes=64)
+        for half in range(B * 2):
+            cols = slice(2 * P * half, 2 * P * (half + 1))
+            quantise_rows(xg_sb[:, half], xg_grouped[:, half], xg_codes[:, cols], xg_scales[:, cols])
+
+        pre = keep.tile([P, B * BLOCKS, G], F32)
+        gates = keep.tile([P, 2, B * BLOCKS, H], F32)
+
+        def gates_of(half):
+            acc = psum.tile([P, 2, G], F32, tag="bank")
+            for i in range(2):
+                cols = slice(P * (2 * half + i), P * (2 * half + i + 1))
+                nc.tensor.matmul_mx(
+                    out=acc[:, i, :],
+                    lhsT=xg_codes[:, cols].bitcast(FP8X4),
+                    lhsT_scale=xg_scales[:, cols],
+                    rhs=w_codes[:].bitcast(FP8X4),
+                    rhs_scale=w_scales[:],
+                    start=True,
+                    stop=True,
+                )
+            blocks = slice(2 * half, 2 * half + 2)
+            nc.vector.tensor_tensor(
+                out=pre[:, blocks, :],
+                in0=acc[:],
+                in1=bias_all[:].unsqueeze(1).to_broadcast([P, 2, G]),
+                op=ADD,
+            )
+            nc.scalar.activation(
+                out=gates[:, :, blocks, :].rearrange("p g i c -> p i g c"),
+                in_=pre[:, blocks, :].rearrange("p i (g c) -> p i g c", g=2),
+                func=SIGMOID,
+            )
+
+        gates_of(0)
+        gates_of(1)
+
+        s_grouped = keep.tile([P, 2, 2, P, PACK], BF16, align_bytes=64)
+        s_codes = keep.tile([P, N], U32, align_bytes=64)
+        s_scales = keep.tile([P, N], U8, align_bytes=64)
+        for half in range(2):
+            cols = slice(2 * P * half, 2 * P * (half + 1))
+            quantise_rows(
+                s_sb[:, 2 * half : 2 * half + 2, :], s_grouped[:, half], s_codes[:, cols], s_scales[:, cols]
+            )
+
+        cand = keep.tile([P, B * BLOCKS, G], F32)
+        x_grouped = keep.tile([P, B, H, PACK], BF16, align_bytes=64)
+        x_codes = keep.tile([P, B * H], U32, align_bytes=64)
+        x_scales = keep.tile([P, B * H], U8, align_bytes=64)
+        nc.vector.tensor_copy(out=x_grouped[:], in_=x_sb[:].rearrange("p (b t) c -> p b c t", b=B))
+        nc.vector.quantize_mx(
+            out=x_codes[:].bitcast(FP8X4),
+            scales=x_scales[:],
+            in_=x_grouped[:].rearrange("p b c t -> p (b c t)"),
+        )
+        nc.scalar.copy(out=cand[:, :, 0:H], in_=x_sb[:])
+
+        gates_of(2)
+        gates_of(3)
+
+        c1 = keep.tile([P, B, BLOCKS, G], F32)
+        for half in range(2):
+            hop = psum.tile([P, 2, B, H], F32, tag="bank")
+            for i in range(2):
+                cols = slice(P * (2 * half + i), P * (2 * half + i + 1))
+                nc.tensor.matmul_mx(
+                    out=hop[:, i].rearrange("p b c -> p (b c)"),
+                    lhsT=s_codes[:, cols].bitcast(FP8X4),
+                    lhsT_scale=s_scales[:, cols],
+                    rhs=x_codes[:].bitcast(FP8X4),
+                    rhs_scale=x_scales[:],
+                    start=True,
+                    stop=True,
+                )
+            copy = nc.scalar.copy if half == 0 else nc.vector.tensor_copy
+            copy(
+                out=c1[:, :, 2 * half : 2 * half + 2, 0:H],
+                in_=hop[:].rearrange("p i b c -> p b i c"),
+            )
+        for b in range(B):
+            nc.sync.dma_start(
+                out=out_2[b].rearrange("(p j) c -> p j c", j=BLOCKS)[:, :, 0:H],
+                in_=c1[:, b, :, 0:H],
+            )
+
+        zs_grouped = keep.tile([P, B, H, PACK], BF16, align_bytes=64)
+        zs_codes = keep.tile([P, B * H], U32, align_bytes=64)
+        zs_scales = keep.tile([P, B * H], U8, align_bytes=64)
+        for b in range(B):
+            blocks = slice(BLOCKS * b, BLOCKS * (b + 1))
+            cols_b = slice(H * b, H * (b + 1))
+            nc.sync.dma_start(
+                out=out_0[b].rearrange("(u p e) c -> p u e c", u=2, e=2),
+                in_=gates[:, 1, blocks, :].rearrange("p (u e) c -> p u e c", u=2),
+            )
+            nc.vector.tensor_tensor(
+                out=zs_grouped[:, b],
+                in0=gates[:, 0, blocks, :].rearrange("p t c -> p c t"),
+                in1=state_sb[:, blocks, :].rearrange("p t c -> p c t"),
+                op=MULT,
+            )
+            nc.vector.tensor_tensor(
+                out=cand[:, blocks, H:G],
+                in0=gates[:, 0, blocks, :],
+                in1=state_sb[:, blocks, :],
+                op=MULT,
+            )
+            nc.vector.quantize_mx(
+                out=zs_codes[:, cols_b].bitcast(FP8X4),
+                scales=zs_scales[:, cols_b],
+                in_=zs_grouped[:, b].rearrange("p c t -> p (c t)"),
+            )
+            nc.sync.dma_start(
+                out=out_1[b].rearrange("(u p e) c -> p u e c", u=2, e=2),
+                in_=cand[:, blocks, :].rearrange("p (u e) c -> p u e c", u=2),
+            )
+            for half in range(2):
+                hop = psum.tile([P, 2, H], F32, tag="bank")
+                for i in range(2):
+                    cols = slice(P * (2 * half + i), P * (2 * half + i + 1))
+                    nc.tensor.matmul_mx(
+                        out=hop[:, i, :],
+                        lhsT=s_codes[:, cols].bitcast(FP8X4),
+                        lhsT_scale=s_scales[:, cols],
+                        rhs=zs_codes[:, cols_b].bitcast(FP8X4),
+                        rhs_scale=zs_scales[:, cols_b],
+                        start=True,
+                        stop=True,
+                    )
+                copy = nc.scalar.copy if half == 0 else nc.vector.tensor_copy
+                copy(out=c1[:, b, 2 * half : 2 * half + 2, H:G], in_=hop[:])
+            nc.sync.dma_start(
+                out=out_2[b].rearrange("(p j) c -> p j c", j=BLOCKS)[:, :, H:G],
+                in_=c1[:, b, :, H:G],
+            )

@@ -13,12 +13,11 @@ SIGMOID = mybir.ActivationFunctionType.Sigmoid
 P = 128
 PACK = 4
 B = 2
-N = 512
+K = 512
 H = 128
 G = 2 * H
-BLOCKS = N // P
 
-FLOPS = 2 * B * N * N * G + 2 * B * N * N * G
+FLOPS = 2 * (B * K) * K * G + 2 * B * K * K * G
 
 
 def tile_agcrncell_pb_s_kernel(
@@ -26,214 +25,202 @@ def tile_agcrncell_pb_s_kernel(
 ):
     nc = tc.nc
     with tc.tile_pool(name="keep", bufs=1) as keep, tc.psum_pool(name="psum", bufs=8) as psum:
-        xg_sb = keep.tile([P, B * 2, 2, N], BF16)
+        xg_sb = keep.tile([P, B, PACK, K], BF16)
         w_sb = keep.tile([P, PACK, G], BF16)
-        s_sb = keep.tile([P, BLOCKS, N], BF16)
-        x_sb = keep.tile([P, B * BLOCKS, H], BF16)
-        state_sb = keep.tile([P, B * BLOCKS, H], BF16)
+        s_sb = keep.tile([P, PACK, K], BF16)
+        x_sb = keep.tile([P, B, PACK, H], BF16)
+        state_sb = keep.tile([P, B, PACK, H], BF16)
         bias_row = keep.tile([P, G], BF16)
-
-        nc.vector.memset(bias_row[:], 0.0)
-        nc.scalar.dma_start(out=bias_row[0:1, :], in_=b_gate.unsqueeze(0))
-
-        def load_xg(b, u):
-            nc.sync.dma_start(
-                out=xg_sb[:, 2 * b + u],
-                in_=xg[b].rearrange("(u p e) k -> u p e k", u=2, e=2)[u],
-            )
-
-        load_xg(0, 0)
-        load_xg(0, 1)
-        nc.sync.dma_start(
-            out=w_sb[:].rearrange("p (u e) c -> p u e c", u=2),
-            in_=W_gate.rearrange("(u p e) c -> p u e c", u=2, e=2),
-        )
-        load_xg(1, 0)
-        load_xg(1, 1)
-        nc.sync.dma_start(out=s_sb[:], in_=supports.rearrange("(p j) m -> p j m", j=BLOCKS))
-        nc.sync.dma_start(
-            out=x_sb[:].rearrange("p (h e) c -> p h (e c)", e=2),
-            in_=x.rearrange("b (u p e) c -> p (b u) (e c)", u=2, e=2),
-        )
-        nc.sync.dma_start(
-            out=state_sb[:].rearrange("p (h e) c -> p h (e c)", e=2),
-            in_=state.rearrange("b (u p e) c -> p (b u) (e c)", u=2, e=2),
-        )
-
         ident = keep.tile([P, P], F32)
-        make_identity(nc, ident[:])
         ones = keep.tile([P, P], BF16)
-        nc.vector.memset(ones[:], 1.0)
         warm_in = keep.tile([P, 1], F32)
         warm_out = keep.tile([P, 1], F32)
-        nc.vector.memset(warm_in[:], 0.0)
-        nc.scalar.activation(out=warm_out[:], in_=warm_in[:], func=SIGMOID)
-
-        bias_ps = psum.tile([P, G], F32, tag="bank")
-        nc.tensor.matmul(out=bias_ps[:], lhsT=ones[:], rhs=bias_row[:], start=True, stop=True)
         bias_all = keep.tile([P, G], F32)
-        nc.scalar.copy(out=bias_all[:], in_=bias_ps[:])
 
         w_grouped = keep.tile([P, G, PACK], BF16, align_bytes=64)
         w_codes = keep.tile([P, G], U32, align_bytes=64)
         w_scales = keep.tile([P, G], U8, align_bytes=64)
-        nc.vector.tensor_copy(out=w_grouped[:], in_=w_sb[:].rearrange("p t c -> p c t"))
-        nc.vector.quantize_mx(
-            out=w_codes[:].bitcast(FP8X4),
-            scales=w_scales[:],
-            in_=w_grouped[:].rearrange("p c t -> p (c t)"),
-        )
+        xg_grouped = keep.tile([P, B, 2, 2, P, PACK], BF16, align_bytes=64)
+        xg_codes = keep.tile([P, B, PACK * P], U32, align_bytes=64)
+        xg_scales = keep.tile([P, B, PACK * P], U8, align_bytes=64)
+        s_grouped = keep.tile([P, 2, 2, P, PACK], BF16, align_bytes=64)
+        s_codes = keep.tile([P, PACK * P], U32, align_bytes=64)
+        s_scales = keep.tile([P, PACK * P], U8, align_bytes=64)
+        x_grouped = keep.tile([P, B, H, PACK], BF16, align_bytes=64)
+        x_codes = keep.tile([P, B * H], U32, align_bytes=64)
+        x_scales = keep.tile([P, B * H], U8, align_bytes=64)
+        zs_grouped = keep.tile([P, B, H, PACK], BF16, align_bytes=64)
+        zs_codes = keep.tile([P, B, H], U32, align_bytes=64)
+        zs_scales = keep.tile([P, B, H], U8, align_bytes=64)
+
+        pre = keep.tile([P, 2, B, PACK, H], F32)
+        gates = keep.tile([P, 2, B, PACK, H], F32)
+        cand = keep.tile([P, B, PACK, G], F32)
+        c1 = keep.tile([P, B, PACK, G], F32)
+
+        nc.vector.memset(bias_row[:], 0.0)
+        nc.sync.dma_start(out=bias_row[0:1, :], in_=b_gate.unsqueeze(0))
+
+        def load_xg(b, pair):
+            blocks = slice(2 * pair, 2 * pair + 2)
+            nc.sync.dma_start(
+                out=xg_sb[:, b, blocks, :],
+                in_=xg[b].rearrange("(p j) k -> p j k", j=PACK)[:, blocks, :],
+            )
+
+        nc.sync.dma_start(out=x_sb[:], in_=x.rearrange("b (p j) c -> p b j c", j=PACK))
+        load_xg(0, 0)
+        nc.sync.dma_start(out=w_sb[:], in_=W_gate.rearrange("(p t) c -> p t c", t=PACK))
+        load_xg(0, 1)
+        load_xg(1, 0)
+        load_xg(1, 1)
+        nc.sync.dma_start(out=s_sb[:], in_=supports.rearrange("(p j) m -> p j m", j=PACK))
+        nc.sync.dma_start(out=state_sb[:], in_=state.rearrange("b (p j) c -> p b j c", j=PACK))
+
+        make_identity(nc, ident[:])
+        nc.vector.memset(ones[:], 1.0)
+        nc.vector.memset(warm_in[:], 0.0)
+        nc.scalar.activation(out=warm_out[:], in_=warm_in[:], func=SIGMOID)
+        bias_ps = psum.tile([P, G], F32, tag="bank")
+        nc.tensor.matmul(out=bias_ps[:], lhsT=ones[:], rhs=bias_row[:], start=True, stop=True)
+        nc.scalar.copy(out=bias_all[:], in_=bias_ps[:])
+
+        def quantise_columns(raw, grouped, codes, scales):
+            nc.vector.tensor_copy(out=grouped, in_=raw.rearrange("p t c -> p c t"))
+            nc.vector.quantize_mx(
+                out=codes.bitcast(FP8X4), scales=scales, in_=grouped.rearrange("p c t -> p (c t)")
+            )
 
         def quantise_rows(rows, grouped, codes, scales):
             bank = psum.tile([P, 2, 2, P], F32, tag="bank")
             for i in range(2):
-                words = rows[:, i, :].bitcast(F32)
+                words = rows[:, i, :].bitcast(F32).rearrange("r (p u) -> r u p", u=2)
                 for u in range(2):
-                    nc.tensor.transpose(bank[:, i, u, :], words[:, P * u : P * (u + 1)], ident[:])
-            nc.scalar.copy(
-                out=grouped.bitcast(F32), in_=bank[:].rearrange("p i u r -> p i r u")
-            )
+                    nc.tensor.transpose(bank[:, i, u, :], words[:, u, :], ident[:])
+            nc.scalar.copy(out=grouped.bitcast(F32), in_=bank[:].rearrange("p i u r -> p i r u"))
             nc.vector.quantize_mx(
-                out=codes.bitcast(FP8X4),
-                scales=scales,
-                in_=grouped.rearrange("p i r t -> p (i r t)"),
+                out=codes.bitcast(FP8X4), scales=scales, in_=grouped.rearrange("p i r t -> p (i r t)")
             )
 
-        xg_grouped = keep.tile([P, B * 2, 2, P, PACK], BF16, align_bytes=64)
-        xg_codes = keep.tile([P, B * N], U32, align_bytes=64)
-        xg_scales = keep.tile([P, B * N], U8, align_bytes=64)
-        for half in range(B * 2):
-            cols = slice(2 * P * half, 2 * P * (half + 1))
-            quantise_rows(xg_sb[:, half], xg_grouped[:, half], xg_codes[:, cols], xg_scales[:, cols])
+        def pair_columns(pair):
+            return slice(2 * P * pair, 2 * P * (pair + 1))
 
-        pre = keep.tile([P, B * BLOCKS, G], F32)
-        gates = keep.tile([P, 2, B * BLOCKS, H], F32)
+        def product(out, rows_codes, rows_scales, block, rhs_codes, rhs_scales):
+            cols = slice(P * block, P * (block + 1))
+            nc.tensor.matmul_mx(
+                out=out,
+                lhsT=rows_codes[:, cols].bitcast(FP8X4),
+                lhsT_scale=rows_scales[:, cols],
+                rhs=rhs_codes.bitcast(FP8X4),
+                rhs_scale=rhs_scales,
+                start=True,
+                stop=True,
+            )
 
-        def gates_of(half):
+        def gate_sums(b, pair):
             acc = psum.tile([P, 2, G], F32, tag="bank")
             for i in range(2):
-                cols = slice(P * (2 * half + i), P * (2 * half + i + 1))
-                nc.tensor.matmul_mx(
-                    out=acc[:, i, :],
-                    lhsT=xg_codes[:, cols].bitcast(FP8X4),
-                    lhsT_scale=xg_scales[:, cols],
-                    rhs=w_codes[:].bitcast(FP8X4),
-                    rhs_scale=w_scales[:],
-                    start=True,
-                    stop=True,
-                )
-            blocks = slice(2 * half, 2 * half + 2)
+                product(acc[:, i, :], xg_codes[:, b], xg_scales[:, b], 2 * pair + i, w_codes[:], w_scales[:])
+            return acc
+
+        def gate(acc, g, b, pair):
+            blocks = slice(2 * pair, 2 * pair + 2)
+            cols = slice(H * g, H * (g + 1))
             nc.vector.tensor_tensor(
-                out=pre[:, blocks, :],
-                in0=acc[:],
-                in1=bias_all[:].unsqueeze(1).to_broadcast([P, 2, G]),
+                out=pre[:, g, b, blocks, :],
+                in0=acc[:, :, cols],
+                in1=bias_all[:, cols].unsqueeze(1).to_broadcast([P, 2, H]),
                 op=ADD,
             )
-            nc.scalar.activation(
-                out=gates[:, :, blocks, :].rearrange("p g i c -> p i g c"),
-                in_=pre[:, blocks, :].rearrange("p i (g c) -> p i g c", g=2),
-                func=SIGMOID,
+            nc.scalar.activation(out=gates[:, g, b, blocks, :], in_=pre[:, g, b, blocks, :], func=SIGMOID)
+
+        nc.scalar.copy(out=cand[:, :, :, 0:H], in_=x_sb[:])
+        for b in range(B):
+            nc.sync.dma_start(
+                out=out_1[b].rearrange("(p j) c -> p j c", j=PACK)[:, :, 0:H], in_=cand[:, b, :, 0:H]
             )
-
-        gates_of(0)
-        gates_of(1)
-
-        s_grouped = keep.tile([P, 2, 2, P, PACK], BF16, align_bytes=64)
-        s_codes = keep.tile([P, N], U32, align_bytes=64)
-        s_scales = keep.tile([P, N], U8, align_bytes=64)
-        for half in range(2):
-            cols = slice(2 * P * half, 2 * P * (half + 1))
-            quantise_rows(
-                s_sb[:, 2 * half : 2 * half + 2, :], s_grouped[:, half], s_codes[:, cols], s_scales[:, cols]
-            )
-
-        cand = keep.tile([P, B * BLOCKS, G], F32)
-        x_grouped = keep.tile([P, B, H, PACK], BF16, align_bytes=64)
-        x_codes = keep.tile([P, B * H], U32, align_bytes=64)
-        x_scales = keep.tile([P, B * H], U8, align_bytes=64)
-        nc.vector.tensor_copy(out=x_grouped[:], in_=x_sb[:].rearrange("p (b t) c -> p b c t", b=B))
+        nc.vector.tensor_copy(out=x_grouped[:], in_=x_sb[:].rearrange("p b t c -> p b c t"))
         nc.vector.quantize_mx(
             out=x_codes[:].bitcast(FP8X4),
             scales=x_scales[:],
             in_=x_grouped[:].rearrange("p b c t -> p (b c t)"),
         )
-        nc.scalar.copy(out=cand[:, :, 0:H], in_=x_sb[:])
 
-        gates_of(2)
-        gates_of(3)
-
-        c1 = keep.tile([P, B, BLOCKS, G], F32)
-        for half in range(2):
-            hop = psum.tile([P, 2, B, H], F32, tag="bank")
-            for i in range(2):
-                cols = slice(P * (2 * half + i), P * (2 * half + i + 1))
-                nc.tensor.matmul_mx(
-                    out=hop[:, i].rearrange("p b c -> p (b c)"),
-                    lhsT=s_codes[:, cols].bitcast(FP8X4),
-                    lhsT_scale=s_scales[:, cols],
-                    rhs=x_codes[:].bitcast(FP8X4),
-                    rhs_scale=x_scales[:],
-                    start=True,
-                    stop=True,
+        quantise_columns(w_sb[:], w_grouped[:], w_codes[:], w_scales[:])
+        for b in range(B):
+            for pair in range(2):
+                cols = pair_columns(pair)
+                quantise_rows(
+                    xg_sb[:, b, 2 * pair : 2 * pair + 2, :],
+                    xg_grouped[:, b, pair],
+                    xg_codes[:, b, cols],
+                    xg_scales[:, b, cols],
                 )
-            copy = nc.scalar.copy if half == 0 else nc.vector.tensor_copy
-            copy(
-                out=c1[:, :, 2 * half : 2 * half + 2, 0:H],
-                in_=hop[:].rearrange("p i b c -> p b i c"),
-            )
-        for b in range(B):
-            nc.sync.dma_start(
-                out=out_2[b].rearrange("(p j) c -> p j c", j=BLOCKS)[:, :, 0:H],
-                in_=c1[:, b, :, 0:H],
-            )
+        sums = {}
 
-        zs_grouped = keep.tile([P, B, H, PACK], BF16, align_bytes=64)
-        zs_codes = keep.tile([P, B * H], U32, align_bytes=64)
-        zs_scales = keep.tile([P, B * H], U8, align_bytes=64)
-        for b in range(B):
-            blocks = slice(BLOCKS * b, BLOCKS * (b + 1))
-            cols_b = slice(H * b, H * (b + 1))
-            nc.sync.dma_start(
-                out=out_0[b].rearrange("(u p e) c -> p u e c", u=2, e=2),
-                in_=gates[:, 1, blocks, :].rearrange("p (u e) c -> p u e c", u=2),
-            )
+        def z_of(b):
+            for pair in range(2):
+                sums[(b, pair)] = gate_sums(b, pair)
+                gate(sums[(b, pair)], 0, b, pair)
+
+        def hop_of_zs(b):
             nc.vector.tensor_tensor(
                 out=zs_grouped[:, b],
-                in0=gates[:, 0, blocks, :].rearrange("p t c -> p c t"),
-                in1=state_sb[:, blocks, :].rearrange("p t c -> p c t"),
-                op=MULT,
-            )
-            nc.vector.tensor_tensor(
-                out=cand[:, blocks, H:G],
-                in0=gates[:, 0, blocks, :],
-                in1=state_sb[:, blocks, :],
+                in0=gates[:, 0, b].rearrange("p t c -> p c t"),
+                in1=state_sb[:, b].rearrange("p t c -> p c t"),
                 op=MULT,
             )
             nc.vector.quantize_mx(
-                out=zs_codes[:, cols_b].bitcast(FP8X4),
-                scales=zs_scales[:, cols_b],
+                out=zs_codes[:, b].bitcast(FP8X4),
+                scales=zs_scales[:, b],
                 in_=zs_grouped[:, b].rearrange("p c t -> p (c t)"),
             )
-            nc.sync.dma_start(
-                out=out_1[b].rearrange("(u p e) c -> p u e c", u=2, e=2),
-                in_=cand[:, blocks, :].rearrange("p (u e) c -> p u e c", u=2),
-            )
-            for half in range(2):
+            for pair in range(2):
                 hop = psum.tile([P, 2, H], F32, tag="bank")
                 for i in range(2):
-                    cols = slice(P * (2 * half + i), P * (2 * half + i + 1))
-                    nc.tensor.matmul_mx(
-                        out=hop[:, i, :],
-                        lhsT=s_codes[:, cols].bitcast(FP8X4),
-                        lhsT_scale=s_scales[:, cols],
-                        rhs=zs_codes[:, cols_b].bitcast(FP8X4),
-                        rhs_scale=zs_scales[:, cols_b],
-                        start=True,
-                        stop=True,
-                    )
-                copy = nc.scalar.copy if half == 0 else nc.vector.tensor_copy
-                copy(out=c1[:, b, 2 * half : 2 * half + 2, H:G], in_=hop[:])
+                    product(hop[:, i, :], s_codes, s_scales, 2 * pair + i, zs_codes[:, b], zs_scales[:, b])
+                copy = nc.scalar.copy if pair == 0 else nc.vector.tensor_copy
+                copy(out=c1[:, b, 2 * pair : 2 * pair + 2, H:G], in_=hop[:])
             nc.sync.dma_start(
-                out=out_2[b].rearrange("(p j) c -> p j c", j=BLOCKS)[:, :, H:G],
-                in_=c1[:, b, :, H:G],
+                out=out_2[b].rearrange("(p j) c -> p j c", j=PACK)[:, :, H:G], in_=c1[:, b, :, H:G]
             )
+
+        def rest_of(b):
+            for pair in range(2):
+                gate(sums[(b, pair)], 1, b, pair)
+            nc.sync.dma_start(out=out_0[b].rearrange("(p j) c -> p j c", j=PACK), in_=gates[:, 1, b])
+            nc.vector.tensor_tensor(
+                out=cand[:, b, :, H:G], in0=gates[:, 0, b], in1=state_sb[:, b], op=MULT
+            )
+            nc.sync.dma_start(
+                out=out_1[b].rearrange("(p j) c -> p j c", j=PACK)[:, :, H:G], in_=cand[:, b, :, H:G]
+            )
+
+        def hop_of_x():
+            for pair in range(2):
+                hop = psum.tile([P, 2, B, H], F32, tag="bank")
+                for i in range(2):
+                    product(
+                        hop[:, i].rearrange("p b c -> p (b c)"), s_codes, s_scales, 2 * pair + i, x_codes[:], x_scales[:]
+                    )
+                copy = nc.scalar.copy if pair == 0 else nc.vector.tensor_copy
+                copy(
+                    out=c1[:, :, 2 * pair : 2 * pair + 2, 0:H], in_=hop[:].rearrange("p i b c -> p b i c")
+                )
+            for b in range(B):
+                nc.sync.dma_start(
+                    out=out_2[b].rearrange("(p j) c -> p j c", j=PACK)[:, :, 0:H], in_=c1[:, b, :, 0:H]
+                )
+
+        z_of(0)
+        rest_of(0)
+        for pair in range(2):
+            cols = pair_columns(pair)
+            quantise_rows(
+                s_sb[:, 2 * pair : 2 * pair + 2, :], s_grouped[:, pair], s_codes[:, cols], s_scales[:, cols]
+            )
+        hop_of_x()
+        hop_of_zs(0)
+        z_of(1)
+        rest_of(1)
+        hop_of_zs(1)

@@ -189,7 +189,7 @@ def tile_agcrncell_pb_s_kernel(
             for pair in range(2):
                 gate(sums[(b, pair)], 1, b, pair)
             nc.sync.dma_start(out=out_0[b].rearrange("(p j) c -> p j c", j=PACK), in_=gates[:, 1, b])
-            nc.vector.tensor_tensor(
+            nc.gpsimd.tensor_tensor(
                 out=cand[:, b, :, H:G], in0=gates[:, 0, b], in1=state_sb[:, b], op=MULT
             )
             nc.sync.dma_start(

@@ -163,7 +163,7 @@ def tile_agcrncell_pb_s_kernel(
                 sums[(b, pair)] = gate_sums(b, pair)
                 gate(sums[(b, pair)], 0, b, pair)
 
-        def hop_of_zs(b):
+        def quantise_zs(b):
             nc.vector.tensor_tensor(
                 out=zs_grouped[:, b],
                 in0=gates[:, 0, b].rearrange("p t c -> p c t"),
@@ -175,6 +175,8 @@ def tile_agcrncell_pb_s_kernel(
                 scales=zs_scales[:, b],
                 in_=zs_grouped[:, b].rearrange("p c t -> p (c t)"),
             )
+
+        def hop_of_zs(b):
             for pair in range(2):
                 hop = psum.tile([P, 2, H], F32, tag="bank")
                 for i in range(2):
@@ -189,7 +191,7 @@ def tile_agcrncell_pb_s_kernel(
             for pair in range(2):
                 gate(sums[(b, pair)], 1, b, pair)
             nc.sync.dma_start(out=out_0[b].rearrange("(p j) c -> p j c", j=PACK), in_=gates[:, 1, b])
-            nc.gpsimd.tensor_tensor(
+            nc.vector.tensor_tensor(
                 out=cand[:, b, :, H:G], in0=gates[:, 0, b], in1=state_sb[:, b], op=MULT
             )
             nc.sync.dma_start(
@@ -203,8 +205,7 @@ def tile_agcrncell_pb_s_kernel(
                     product(
                         hop[:, i].rearrange("p b c -> p (b c)"), s_codes, s_scales, 2 * pair + i, x_codes[:], x_scales[:]
                     )
-                copy = nc.scalar.copy if pair == 0 else nc.vector.tensor_copy
-                copy(
+                nc.scalar.copy(
                     out=c1[:, :, 2 * pair : 2 * pair + 2, 0:H], in_=hop[:].rearrange("p i b c -> p b i c")
                 )
             for b in range(B):
@@ -213,14 +214,16 @@ def tile_agcrncell_pb_s_kernel(
                 )
 
         z_of(0)
+        quantise_zs(0)
         rest_of(0)
+        z_of(1)
+        quantise_zs(1)
         for pair in range(2):
             cols = pair_columns(pair)
             quantise_rows(
                 s_sb[:, 2 * pair : 2 * pair + 2, :], s_grouped[:, pair], s_codes[:, cols], s_scales[:, cols]
             )
-        hop_of_x()
         hop_of_zs(0)
-        z_of(1)
+        hop_of_x()
         rest_of(1)
         hop_of_zs(1)

@@ -183,9 +183,7 @@ def tile_agcrncell_pb_s_kernel(
                     product(hop[:, i, :], s_codes, s_scales, 2 * pair + i, zs_codes[:, b], zs_scales[:, b])
                 copy = nc.scalar.copy if pair == 0 else nc.vector.tensor_copy
                 copy(out=c1[:, b, 2 * pair : 2 * pair + 2, H:G], in_=hop[:])
-            nc.sync.dma_start(
-                out=out_2[b].rearrange("(p j) c -> p j c", j=PACK)[:, :, H:G], in_=c1[:, b, :, H:G]
-            )
+            nc.sync.dma_start(out=out_2[b].rearrange("(p j) c -> p j c", j=PACK), in_=c1[:, b])
 
         def rest_of(b):
             for pair in range(2):
@@ -208,10 +206,6 @@ def tile_agcrncell_pb_s_kernel(
                 nc.scalar.copy(
                     out=c1[:, :, 2 * pair : 2 * pair + 2, 0:H], in_=hop[:].rearrange("p i b c -> p b i c")
                 )
-            for b in range(B):
-                nc.sync.dma_start(
-                    out=out_2[b].rearrange("(p j) c -> p j c", j=PACK)[:, :, 0:H], in_=c1[:, b, :, 0:H]
-                )
 
         z_of(0)
         quantise_zs(0)
@@ -223,7 +217,7 @@ def tile_agcrncell_pb_s_kernel(
             quantise_rows(
                 s_sb[:, 2 * pair : 2 * pair + 2, :], s_grouped[:, pair], s_codes[:, cols], s_scales[:, cols]
             )
-        hop_of_zs(0)
         hop_of_x()
+        hop_of_zs(0)
         rest_of(1)
         hop_of_zs(1)

@@ -163,13 +163,16 @@ def tile_agcrncell_pb_s_kernel(
                 sums[(b, pair)] = gate_sums(b, pair)
                 gate(sums[(b, pair)], 0, b, pair)
 
-        def quantise_zs(b):
+        def product_in_float32(b):
             nc.vector.tensor_tensor(
-                out=zs_grouped[:, b],
-                in0=gates[:, 0, b].rearrange("p t c -> p c t"),
-                in1=state_sb[:, b].rearrange("p t c -> p c t"),
-                op=MULT,
+                out=cand[:, b, :, H:G], in0=gates[:, 0, b], in1=state_sb[:, b], op=MULT
             )
+            nc.sync.dma_start(
+                out=out_1[b].rearrange("(p j) c -> p j c", j=PACK)[:, :, H:G], in_=cand[:, b, :, H:G]
+            )
+
+        def quantise_zs(b):
+            nc.vector.tensor_copy(out=zs_grouped[:, b], in_=cand[:, b, :, H:G].rearrange("p t c -> p c t"))
             nc.vector.quantize_mx(
                 out=zs_codes[:, b].bitcast(FP8X4),
                 scales=zs_scales[:, b],
@@ -185,16 +188,10 @@ def tile_agcrncell_pb_s_kernel(
                 copy(out=c1[:, b, 2 * pair : 2 * pair + 2, H:G], in_=hop[:])
             nc.sync.dma_start(out=out_2[b].rearrange("(p j) c -> p j c", j=PACK), in_=c1[:, b])
 
-        def rest_of(b):
+        def r_of(b):
             for pair in range(2):
                 gate(sums[(b, pair)], 1, b, pair)
             nc.sync.dma_start(out=out_0[b].rearrange("(p j) c -> p j c", j=PACK), in_=gates[:, 1, b])
-            nc.vector.tensor_tensor(
-                out=cand[:, b, :, H:G], in0=gates[:, 0, b], in1=state_sb[:, b], op=MULT
-            )
-            nc.sync.dma_start(
-                out=out_1[b].rearrange("(p j) c -> p j c", j=PACK)[:, :, H:G], in_=cand[:, b, :, H:G]
-            )
 
         def hop_of_x():
             for pair in range(2):
@@ -208,9 +205,11 @@ def tile_agcrncell_pb_s_kernel(
                 )
 
         z_of(0)
+        product_in_float32(0)
         quantise_zs(0)
-        rest_of(0)
+        r_of(0)
         z_of(1)
+        product_in_float32(1)
         quantise_zs(1)
         for pair in range(2):
             cols = pair_columns(pair)
@@ -219,5 +218,5 @@ def tile_agcrncell_pb_s_kernel(
             )
         hop_of_x()
         hop_of_zs(0)
-        rest_of(1)
+        r_of(1)
         hop_of_zs(1)

@@ -16,6 +16,11 @@ B = 2
 K = 512
 H = 128
 G = 2 * H
+Z, R = 0, 1
+PAIR = 1
+PAIRS = PACK // PAIR
+HALVES = 2
+BANKS = 8
 
 FLOPS = 2 * (B * K) * K * G + 2 * B * K * K * G
 
@@ -24,7 +29,7 @@ def tile_agcrncell_pb_s_kernel(
     tc, xg, W_gate, b_gate, x, state, supports, out_0, out_1, out_2
 ):
     nc = tc.nc
-    with tc.tile_pool(name="keep", bufs=1) as keep, tc.psum_pool(name="psum", bufs=8) as psum:
+    with tc.tile_pool(name="keep", bufs=1) as keep, tc.psum_pool(name="psum", bufs=BANKS) as psum:
         xg_sb = keep.tile([P, B, PACK, K], BF16)
         w_sb = keep.tile([P, PACK, G], BF16)
         s_sb = keep.tile([P, PACK, K], BF16)
@@ -40,10 +45,10 @@ def tile_agcrncell_pb_s_kernel(
         w_grouped = keep.tile([P, G, PACK], BF16, align_bytes=64)
         w_codes = keep.tile([P, G], U32, align_bytes=64)
         w_scales = keep.tile([P, G], U8, align_bytes=64)
-        xg_grouped = keep.tile([P, B, 2, 2, P, PACK], BF16, align_bytes=64)
+        xg_grouped = keep.tile([P, B, PAIRS, PAIR, P, PACK], BF16, align_bytes=64)
         xg_codes = keep.tile([P, B, PACK * P], U32, align_bytes=64)
         xg_scales = keep.tile([P, B, PACK * P], U8, align_bytes=64)
-        s_grouped = keep.tile([P, 2, 2, P, PACK], BF16, align_bytes=64)
+        s_grouped = keep.tile([P, PAIRS, PAIR, P, PACK], BF16, align_bytes=64)
         s_codes = keep.tile([P, PACK * P], U32, align_bytes=64)
         s_scales = keep.tile([P, PACK * P], U8, align_bytes=64)
         x_grouped = keep.tile([P, B, H, PACK], BF16, align_bytes=64)
@@ -58,23 +63,26 @@ def tile_agcrncell_pb_s_kernel(
         cand = keep.tile([P, B, PACK, G], F32)
         c1 = keep.tile([P, B, PACK, G], F32)
 
+        def rows_of(dram):
+            return dram.rearrange("(p j) n -> p j n", j=PACK)
+
+        def blocks_of(pair):
+            return slice(PAIR * pair, PAIR * (pair + 1))
+
         nc.vector.memset(bias_row[:], 0.0)
         nc.sync.dma_start(out=bias_row[0:1, :], in_=b_gate.unsqueeze(0))
 
-        def load_xg(b, pair):
-            blocks = slice(2 * pair, 2 * pair + 2)
-            nc.sync.dma_start(
-                out=xg_sb[:, b, blocks, :],
-                in_=xg[b].rearrange("(p j) k -> p j k", j=PACK)[:, blocks, :],
-            )
+        def load_xg(b, half):
+            blocks = slice(2 * half, 2 * half + 2)
+            nc.sync.dma_start(out=xg_sb[:, b, blocks, :], in_=rows_of(xg[b])[:, blocks, :])
 
         nc.sync.dma_start(out=x_sb[:], in_=x.rearrange("b (p j) c -> p b j c", j=PACK))
         load_xg(0, 0)
-        nc.sync.dma_start(out=w_sb[:], in_=W_gate.rearrange("(p t) c -> p t c", t=PACK))
+        nc.sync.dma_start(out=w_sb[:], in_=rows_of(W_gate))
         load_xg(0, 1)
         load_xg(1, 0)
         load_xg(1, 1)
-        nc.sync.dma_start(out=s_sb[:], in_=supports.rearrange("(p j) m -> p j m", j=PACK))
+        nc.sync.dma_start(out=s_sb[:], in_=rows_of(supports))
         nc.sync.dma_start(out=state_sb[:], in_=state.rearrange("b (p j) c -> p b j c", j=PACK))
 
         make_identity(nc, ident[:])
@@ -85,25 +93,19 @@ def tile_agcrncell_pb_s_kernel(
         nc.tensor.matmul(out=bias_ps[:], lhsT=ones[:], rhs=bias_row[:], start=True, stop=True)
         nc.scalar.copy(out=bias_all[:], in_=bias_ps[:])
 
-        def quantise_columns(raw, grouped, codes, scales):
-            nc.vector.tensor_copy(out=grouped, in_=raw.rearrange("p t c -> p c t"))
-            nc.vector.quantize_mx(
-                out=codes.bitcast(FP8X4), scales=scales, in_=grouped.rearrange("p c t -> p (c t)")
-            )
-
         def quantise_rows(rows, grouped, codes, scales):
-            bank = psum.tile([P, 2, 2, P], F32, tag="bank")
-            for i in range(2):
-                words = rows[:, i, :].bitcast(F32).rearrange("r (p u) -> r u p", u=2)
-                for u in range(2):
+            bank = psum.tile([P, PAIR, HALVES, P], F32, tag="bank")
+            for i in range(PAIR):
+                words = rows[:, i, :].bitcast(F32).rearrange("r (p u) -> r u p", u=HALVES)
+                for u in range(HALVES):
                     nc.tensor.transpose(bank[:, i, u, :], words[:, u, :], ident[:])
             nc.scalar.copy(out=grouped.bitcast(F32), in_=bank[:].rearrange("p i u r -> p i r u"))
             nc.vector.quantize_mx(
                 out=codes.bitcast(FP8X4), scales=scales, in_=grouped.rearrange("p i r t -> p (i r t)")
             )
 
-        def pair_columns(pair):
-            return slice(2 * P * pair, 2 * P * (pair + 1))
+        def columns_of(pair):
+            return slice(PAIR * P * pair, PAIR * P * (pair + 1))
 
         def product(out, rows_codes, rows_scales, block, rhs_codes, rhs_scales):
             cols = slice(P * block, P * (block + 1))
@@ -118,27 +120,84 @@ def tile_agcrncell_pb_s_kernel(
             )
 
         def gate_sums(b, pair):
-            acc = psum.tile([P, 2, G], F32, tag="bank")
-            for i in range(2):
-                product(acc[:, i, :], xg_codes[:, b], xg_scales[:, b], 2 * pair + i, w_codes[:], w_scales[:])
+            acc = psum.tile([P, PAIR, G], F32, tag="bank")
+            for i in range(PAIR):
+                product(
+                    acc[:, i, :], xg_codes[:, b], xg_scales[:, b], PAIR * pair + i, w_codes[:], w_scales[:]
+                )
             return acc
 
         def gate(acc, g, b, pair):
-            blocks = slice(2 * pair, 2 * pair + 2)
             cols = slice(H * g, H * (g + 1))
             nc.vector.tensor_tensor(
-                out=pre[:, g, b, blocks, :],
+                out=pre[:, g, b, blocks_of(pair), :],
                 in0=acc[:, :, cols],
-                in1=bias_all[:, cols].unsqueeze(1).to_broadcast([P, 2, H]),
+                in1=bias_all[:, cols].unsqueeze(1).to_broadcast([P, PAIR, H]),
                 op=ADD,
             )
-            nc.scalar.activation(out=gates[:, g, b, blocks, :], in_=pre[:, g, b, blocks, :], func=SIGMOID)
+            nc.scalar.activation(
+                out=gates[:, g, b, blocks_of(pair), :], in_=pre[:, g, b, blocks_of(pair), :], func=SIGMOID
+            )
+
+        sums = {}
+
+        def z_of(b):
+            for pair in range(PAIRS):
+                sums[(b, pair)] = gate_sums(b, pair)
+                gate(sums[(b, pair)], Z, b, pair)
+
+        def r_of(b):
+            for pair in range(PAIRS):
+                gate(sums[(b, pair)], R, b, pair)
+            nc.sync.dma_start(out=rows_of(out_0[b]), in_=gates[:, R, b])
+
+        def z_times_state(b):
+            nc.vector.tensor_tensor(
+                out=cand[:, b, :, H:G], in0=gates[:, Z, b], in1=state_sb[:, b], op=MULT
+            )
+            nc.sync.dma_start(out=rows_of(out_1[b])[:, :, H:G], in_=cand[:, b, :, H:G])
+
+        def quantise_zs(b):
+            nc.vector.tensor_copy(
+                out=zs_grouped[:, b], in_=cand[:, b, :, H:G].rearrange("p t c -> p c t")
+            )
+            nc.vector.quantize_mx(
+                out=zs_codes[:, b].bitcast(FP8X4),
+                scales=zs_scales[:, b],
+                in_=zs_grouped[:, b].rearrange("p c t -> p (c t)"),
+            )
+
+        def hop_of_x():
+            for pair in range(PAIRS):
+                hop = psum.tile([P, PAIR, B, H], F32, tag="bank")
+                for i in range(PAIR):
+                    product(
+                        hop[:, i].rearrange("p b c -> p (b c)"),
+                        s_codes,
+                        s_scales,
+                        PAIR * pair + i,
+                        x_codes[:],
+                        x_scales[:],
+                    )
+                nc.scalar.copy(
+                    out=c1[:, :, blocks_of(pair), 0:H], in_=hop[:].rearrange("p i b c -> p b i c")
+                )
+
+        def hop_of_zs(b):
+            for pair in range(PAIRS):
+                hop = psum.tile([P, PAIR, H], F32, tag="bank")
+                for i in range(PAIR):
+                    product(
+                        hop[:, i, :], s_codes, s_scales, PAIR * pair + i, zs_codes[:, b], zs_scales[:, b]
+                    )
+                copy = nc.scalar.copy if pair % 2 == 0 else nc.vector.tensor_copy
+                copy(out=c1[:, b, blocks_of(pair), H:G], in_=hop[:])
+            nc.sync.dma_start(out=rows_of(out_2[b]), in_=c1[:, b])
+
 
         nc.scalar.copy(out=cand[:, :, :, 0:H], in_=x_sb[:])
         for b in range(B):
-            nc.sync.dma_start(
-                out=out_1[b].rearrange("(p j) c -> p j c", j=PACK)[:, :, 0:H], in_=cand[:, b, :, 0:H]
-            )
+            nc.sync.dma_start(out=rows_of(out_1[b])[:, :, 0:H], in_=cand[:, b, :, 0:H])
         nc.vector.tensor_copy(out=x_grouped[:], in_=x_sb[:].rearrange("p b t c -> p b c t"))
         nc.vector.quantize_mx(
             out=x_codes[:].bitcast(FP8X4),
@@ -146,75 +205,34 @@ def tile_agcrncell_pb_s_kernel(
             in_=x_grouped[:].rearrange("p b c t -> p (b c t)"),
         )
 
-        quantise_columns(w_sb[:], w_grouped[:], w_codes[:], w_scales[:])
+        nc.vector.tensor_copy(out=w_grouped[:], in_=w_sb[:].rearrange("p t c -> p c t"))
+        nc.vector.quantize_mx(
+            out=w_codes[:].bitcast(FP8X4),
+            scales=w_scales[:],
+            in_=w_grouped[:].rearrange("p c t -> p (c t)"),
+        )
         for b in range(B):
-            for pair in range(2):
-                cols = pair_columns(pair)
+            for pair in range(PAIRS):
                 quantise_rows(
-                    xg_sb[:, b, 2 * pair : 2 * pair + 2, :],
+                    xg_sb[:, b, blocks_of(pair), :],
                     xg_grouped[:, b, pair],
-                    xg_codes[:, b, cols],
-                    xg_scales[:, b, cols],
-                )
-        sums = {}
-
-        def z_of(b):
-            for pair in range(2):
-                sums[(b, pair)] = gate_sums(b, pair)
-                gate(sums[(b, pair)], 0, b, pair)
-
-        def product_in_float32(b):
-            nc.vector.tensor_tensor(
-                out=cand[:, b, :, H:G], in0=gates[:, 0, b], in1=state_sb[:, b], op=MULT
-            )
-            nc.sync.dma_start(
-                out=out_1[b].rearrange("(p j) c -> p j c", j=PACK)[:, :, H:G], in_=cand[:, b, :, H:G]
-            )
-
-        def quantise_zs(b):
-            nc.vector.tensor_copy(out=zs_grouped[:, b], in_=cand[:, b, :, H:G].rearrange("p t c -> p c t"))
-            nc.vector.quantize_mx(
-                out=zs_codes[:, b].bitcast(FP8X4),
-                scales=zs_scales[:, b],
-                in_=zs_grouped[:, b].rearrange("p c t -> p (c t)"),
-            )
-
-        def hop_of_zs(b):
-            for pair in range(2):
-                hop = psum.tile([P, 2, H], F32, tag="bank")
-                for i in range(2):
-                    product(hop[:, i, :], s_codes, s_scales, 2 * pair + i, zs_codes[:, b], zs_scales[:, b])
-                copy = nc.scalar.copy if pair == 0 else nc.vector.tensor_copy
-                copy(out=c1[:, b, 2 * pair : 2 * pair + 2, H:G], in_=hop[:])
-            nc.sync.dma_start(out=out_2[b].rearrange("(p j) c -> p j c", j=PACK), in_=c1[:, b])
-
-        def r_of(b):
-            for pair in range(2):
-                gate(sums[(b, pair)], 1, b, pair)
-            nc.sync.dma_start(out=out_0[b].rearrange("(p j) c -> p j c", j=PACK), in_=gates[:, 1, b])
-
-        def hop_of_x():
-            for pair in range(2):
-                hop = psum.tile([P, 2, B, H], F32, tag="bank")
-                for i in range(2):
-                    product(
-                        hop[:, i].rearrange("p b c -> p (b c)"), s_codes, s_scales, 2 * pair + i, x_codes[:], x_scales[:]
-                    )
-                nc.scalar.copy(
-                    out=c1[:, :, 2 * pair : 2 * pair + 2, 0:H], in_=hop[:].rearrange("p i b c -> p b i c")
+                    xg_codes[:, b, columns_of(pair)],
+                    xg_scales[:, b, columns_of(pair)],
                 )
 
         z_of(0)
-        product_in_float32(0)
+        z_times_state(0)
         quantise_zs(0)
         r_of(0)
         z_of(1)
-        product_in_float32(1)
+        z_times_state(1)
         quantise_zs(1)
-        for pair in range(2):
-            cols = pair_columns(pair)
+        for pair in range(PAIRS):
             quantise_rows(
-                s_sb[:, 2 * pair : 2 * pair + 2, :], s_grouped[:, pair], s_codes[:, cols], s_scales[:, cols]
+                s_sb[:, blocks_of(pair), :],
+                s_grouped[:, pair],
+                s_codes[:, columns_of(pair)],
+                s_scales[:, columns_of(pair)],
             )
         hop_of_x()
         hop_of_zs(0)

@@ -16,9 +16,8 @@ B = 2
 K = 512
 H = 128
 G = 2 * H
-Z, R = 0, 1
-PAIR = 1
-PAIRS = PACK // PAIR
+Z = 0
+PAIR = 2
 HALVES = 2
 BANKS = 8
 
@@ -40,15 +39,15 @@ def tile_agcrncell_pb_s_kernel(
         ones = keep.tile([P, P], BF16)
         warm_in = keep.tile([P, 1], F32)
         warm_out = keep.tile([P, 1], F32)
-        bias_all = keep.tile([P, G], F32)
+        bias = keep.tile([P, H + 1], F32)
 
         w_grouped = keep.tile([P, G, PACK], BF16, align_bytes=64)
         w_codes = keep.tile([P, G], U32, align_bytes=64)
         w_scales = keep.tile([P, G], U8, align_bytes=64)
-        xg_grouped = keep.tile([P, B, PAIRS, PAIR, P, PACK], BF16, align_bytes=64)
+        xg_grouped = keep.tile([P, B, PACK, P, PACK], BF16, align_bytes=64)
         xg_codes = keep.tile([P, B, PACK * P], U32, align_bytes=64)
         xg_scales = keep.tile([P, B, PACK * P], U8, align_bytes=64)
-        s_grouped = keep.tile([P, PAIRS, PAIR, P, PACK], BF16, align_bytes=64)
+        s_grouped = keep.tile([P, PACK, P, PACK], BF16, align_bytes=64)
         s_codes = keep.tile([P, PACK * P], U32, align_bytes=64)
         s_scales = keep.tile([P, PACK * P], U8, align_bytes=64)
         x_grouped = keep.tile([P, B, H, PACK], BF16, align_bytes=64)
@@ -58,57 +57,56 @@ def tile_agcrncell_pb_s_kernel(
         zs_codes = keep.tile([P, B, H], U32, align_bytes=64)
         zs_scales = keep.tile([P, B, H], U8, align_bytes=64)
 
-        pre = keep.tile([P, 2, B, PACK, H], F32)
-        gates = keep.tile([P, 2, B, PACK, H], F32)
+        r_pre = keep.tile([P, B, PACK, H], F32)
+        r = keep.tile([P, B, PACK, H], F32)
+        z_cols = keep.tile([P, B, PACK, P], F32)
         cand = keep.tile([P, B, PACK, G], F32)
         c1 = keep.tile([P, B, PACK, G], F32)
 
         def rows_of(dram):
             return dram.rearrange("(p j) n -> p j n", j=PACK)
 
-        def blocks_of(pair):
-            return slice(PAIR * pair, PAIR * (pair + 1))
+        def pair_of(h):
+            return slice(PAIR * h, PAIR * (h + 1))
 
-        nc.vector.memset(bias_row[:], 0.0)
-        nc.sync.dma_start(out=bias_row[0:1, :], in_=b_gate.unsqueeze(0))
-
-        def load_xg(b, half):
-            blocks = slice(2 * half, 2 * half + 2)
-            nc.sync.dma_start(out=xg_sb[:, b, blocks, :], in_=rows_of(xg[b])[:, blocks, :])
-
-        nc.sync.dma_start(out=x_sb[:], in_=x.rearrange("b (p j) c -> p b j c", j=PACK))
-        load_xg(0, 0)
-        nc.sync.dma_start(out=w_sb[:], in_=rows_of(W_gate))
-        load_xg(0, 1)
-        load_xg(1, 0)
-        load_xg(1, 1)
-        nc.sync.dma_start(out=s_sb[:], in_=rows_of(supports))
-        nc.sync.dma_start(out=state_sb[:], in_=state.rearrange("b (p j) c -> p b j c", j=PACK))
+        def columns_of(first, count):
+            return slice(P * first, P * (first + count))
 
         make_identity(nc, ident[:])
-        nc.vector.memset(ones[:], 1.0)
-        nc.vector.memset(warm_in[:], 0.0)
-        nc.scalar.activation(out=warm_out[:], in_=warm_in[:], func=SIGMOID)
-        bias_ps = psum.tile([P, G], F32, tag="bank")
-        nc.tensor.matmul(out=bias_ps[:], lhsT=ones[:], rhs=bias_row[:], start=True, stop=True)
-        nc.scalar.copy(out=bias_all[:], in_=bias_ps[:])
 
-        def quantise_rows(rows, grouped, codes, scales):
-            bank = psum.tile([P, PAIR, HALVES, P], F32, tag="bank")
-            for i in range(PAIR):
-                words = rows[:, i, :].bitcast(F32).rearrange("r (p u) -> r u p", u=HALVES)
-                for u in range(HALVES):
-                    nc.tensor.transpose(bank[:, i, u, :], words[:, u, :], ident[:])
-            nc.scalar.copy(out=grouped.bitcast(F32), in_=bank[:].rearrange("p i u r -> p i r u"))
-            nc.vector.quantize_mx(
-                out=codes.bitcast(FP8X4), scales=scales, in_=grouped.rearrange("p i r t -> p (i r t)")
-            )
+        def turn(rows, word_order):
+            bank = psum.tile([P, HALVES, P], F32, tag="bank")
+            words = rows.bitcast(F32).rearrange(word_order, u=HALVES)
+            for u in range(HALVES):
+                nc.tensor.transpose(bank[:, u, :], words[:, u, :], ident[:])
+            return bank
 
-        def columns_of(pair):
-            return slice(PAIR * P * pair, PAIR * P * (pair + 1))
+        def collect(bank, grouped):
+            nc.scalar.copy(out=grouped.bitcast(F32), in_=bank[:].rearrange("p u r -> p r u"))
+
+        def turn_xg(b, *blocks):
+            for j in blocks:
+                collect(turn(xg_sb[:, b, j, :], "r (u p) -> r u p"), xg_grouped[:, b, j])
+
+        def turn_s(*blocks):
+            for j in blocks:
+                collect(turn(s_sb[:, j, :], "r (p u) -> r u p"), s_grouped[:, j])
+
+        def quantise(grouped, codes, scales):
+            nc.vector.quantize_mx(out=codes.bitcast(FP8X4), scales=scales, in_=grouped)
+
+        def quantise_pair(h, grouped, codes, scales):
+            cols = columns_of(PAIR * h, PAIR)
+            quantise(grouped[:, pair_of(h)].rearrange("p j r t -> p (j r t)"), codes[:, cols], scales[:, cols])
+
+        def quantise_xg(b, h):
+            quantise_pair(h, xg_grouped[:, b], xg_codes[:, b], xg_scales[:, b])
+
+        def quantise_s(h):
+            quantise_pair(h, s_grouped, s_codes, s_scales)
 
         def product(out, rows_codes, rows_scales, block, rhs_codes, rhs_scales):
-            cols = slice(P * block, P * (block + 1))
+            cols = columns_of(block, 1)
             nc.tensor.matmul_mx(
                 out=out,
                 lhsT=rows_codes[:, cols].bitcast(FP8X4),
@@ -119,122 +117,119 @@ def tile_agcrncell_pb_s_kernel(
                 stop=True,
             )
 
-        def gate_sums(b, pair):
-            acc = psum.tile([P, PAIR, G], F32, tag="bank")
-            for i in range(PAIR):
-                product(
-                    acc[:, i, :], xg_codes[:, b], xg_scales[:, b], PAIR * pair + i, w_codes[:], w_scales[:]
-                )
-            return acc
-
-        def gate(acc, g, b, pair):
-            cols = slice(H * g, H * (g + 1))
-            nc.vector.tensor_tensor(
-                out=pre[:, g, b, blocks_of(pair), :],
-                in0=acc[:, :, cols],
-                in1=bias_all[:, cols].unsqueeze(1).to_broadcast([P, PAIR, H]),
-                op=ADD,
-            )
-            nc.scalar.activation(
-                out=gates[:, g, b, blocks_of(pair), :], in_=pre[:, g, b, blocks_of(pair), :], func=SIGMOID
-            )
-
-        sums = {}
-
         def z_of(b):
-            for pair in range(PAIRS):
-                sums[(b, pair)] = gate_sums(b, pair)
-                gate(sums[(b, pair)], Z, b, pair)
+            acc = psum.tile([P, PACK, P], F32, tag="bank")
+            product(acc[:].rearrange("c j i -> c (j i)"), w_codes, w_scales, Z, xg_codes[:, b], xg_scales[:, b])
+            nc.scalar.activation(out=z_cols[:, b], in_=acc[:], func=SIGMOID, bias=bias[:, H : H + 1])
+
+        def r_sums(b):
+            acc = psum.tile([P, PACK, H], F32, tag="bank")
+            for j in range(PACK):
+                product(acc[:, j, :], xg_codes[:, b], xg_scales[:, b], j, w_codes[:, H:G], w_scales[:, H:G])
+            nc.vector.tensor_tensor(
+                out=r_pre[:, b], in0=acc[:], in1=bias[:, 0:H].unsqueeze(1).to_broadcast([P, PACK, H]), op=ADD
+            )
 
         def r_of(b):
-            for pair in range(PAIRS):
-                gate(sums[(b, pair)], R, b, pair)
-            nc.sync.dma_start(out=rows_of(out_0[b]), in_=gates[:, R, b])
+            nc.scalar.activation(out=r[:, b], in_=r_pre[:, b], func=SIGMOID)
+            nc.sync.dma_start(out=rows_of(out_0[b]), in_=r[:, b])
 
         def z_times_state(b):
-            nc.vector.tensor_tensor(
-                out=cand[:, b, :, H:G], in0=gates[:, Z, b], in1=state_sb[:, b], op=MULT
-            )
+            z_rows = psum.tile([P, PACK, H], F32, tag="bank")
+            for j in range(PACK):
+                nc.tensor.transpose(z_rows[:, j, :], z_cols[:, b, j, :], ident[:])
+            nc.vector.tensor_tensor(out=cand[:, b, :, H:G], in0=z_rows[:], in1=state_sb[:, b], op=MULT)
             nc.sync.dma_start(out=rows_of(out_1[b])[:, :, H:G], in_=cand[:, b, :, H:G])
 
+        def round_zs(b, copy):
+            copy(out=zs_grouped[:, b], in_=cand[:, b, :, H:G].rearrange("p t c -> p c t"))
+
         def quantise_zs(b):
-            nc.vector.tensor_copy(
-                out=zs_grouped[:, b], in_=cand[:, b, :, H:G].rearrange("p t c -> p c t")
-            )
-            nc.vector.quantize_mx(
-                out=zs_codes[:, b].bitcast(FP8X4),
-                scales=zs_scales[:, b],
-                in_=zs_grouped[:, b].rearrange("p c t -> p (c t)"),
-            )
+            quantise(zs_grouped[:, b].rearrange("p c t -> p (c t)"), zs_codes[:, b], zs_scales[:, b])
 
-        def hop_of_x():
-            for pair in range(PAIRS):
-                hop = psum.tile([P, PAIR, B, H], F32, tag="bank")
-                for i in range(PAIR):
-                    product(
-                        hop[:, i].rearrange("p b c -> p (b c)"),
-                        s_codes,
-                        s_scales,
-                        PAIR * pair + i,
-                        x_codes[:],
-                        x_scales[:],
-                    )
-                nc.scalar.copy(
-                    out=c1[:, :, blocks_of(pair), 0:H], in_=hop[:].rearrange("p i b c -> p b i c")
+        def hop_of_x(h, copy):
+            hop = psum.tile([P, PAIR, B, H], F32, tag="bank")
+            for i in range(PAIR):
+                product(
+                    hop[:, i].rearrange("p b c -> p (b c)"), s_codes, s_scales, PAIR * h + i, x_codes[:], x_scales[:]
                 )
+            copy(out=c1[:, :, pair_of(h), 0:H], in_=hop[:].rearrange("p i b c -> p b i c"))
 
-        def hop_of_zs(b):
-            for pair in range(PAIRS):
-                hop = psum.tile([P, PAIR, H], F32, tag="bank")
-                for i in range(PAIR):
-                    product(
-                        hop[:, i, :], s_codes, s_scales, PAIR * pair + i, zs_codes[:, b], zs_scales[:, b]
-                    )
-                copy = nc.scalar.copy if pair % 2 == 0 else nc.vector.tensor_copy
-                copy(out=c1[:, b, blocks_of(pair), H:G], in_=hop[:])
-            nc.sync.dma_start(out=rows_of(out_2[b]), in_=c1[:, b])
+        def hop_of_zs(b, h, copy):
+            hop = psum.tile([P, PAIR, H], F32, tag="bank")
+            for i in range(PAIR):
+                product(hop[:, i, :], s_codes, s_scales, PAIR * h + i, zs_codes[:, b], zs_scales[:, b])
+            copy(out=c1[:, b, pair_of(h), H:G], in_=hop[:])
 
+        def store_c1(h):
+            for b in range(B):
+                nc.sync.dma_start(out=rows_of(out_2[b])[:, pair_of(h), :], in_=c1[:, b, pair_of(h), :])
 
-        nc.scalar.copy(out=cand[:, :, :, 0:H], in_=x_sb[:])
-        for b in range(B):
-            nc.sync.dma_start(out=rows_of(out_1[b])[:, :, 0:H], in_=cand[:, b, :, 0:H])
-        nc.vector.tensor_copy(out=x_grouped[:], in_=x_sb[:].rearrange("p b t c -> p b c t"))
-        nc.vector.quantize_mx(
-            out=x_codes[:].bitcast(FP8X4),
-            scales=x_scales[:],
-            in_=x_grouped[:].rearrange("p b c t -> p (b c t)"),
-        )
+        def load_xg(b, h):
+            nc.sync.dma_start(out=xg_sb[:, b, pair_of(h), :], in_=rows_of(xg[b])[:, pair_of(h), :])
 
-        nc.vector.tensor_copy(out=w_grouped[:], in_=w_sb[:].rearrange("p t c -> p c t"))
-        nc.vector.quantize_mx(
-            out=w_codes[:].bitcast(FP8X4),
-            scales=w_scales[:],
-            in_=w_grouped[:].rearrange("p c t -> p (c t)"),
-        )
-        for b in range(B):
-            for pair in range(PAIRS):
-                quantise_rows(
-                    xg_sb[:, b, blocks_of(pair), :],
-                    xg_grouped[:, b, pair],
-                    xg_codes[:, b, columns_of(pair)],
-                    xg_scales[:, b, columns_of(pair)],
-                )
+        with tc.manual_schedule():
+            nc.vector.memset(warm_in[:], 0.0)
+            nc.vector.memset(bias_row[:], 0.0)
+            nc.vector.memset(ones[:], 1.0)
+            nc.scalar.activation(out=warm_out[:], in_=warm_in[:], func=SIGMOID)
 
-        z_of(0)
-        z_times_state(0)
-        quantise_zs(0)
-        r_of(0)
-        z_of(1)
-        z_times_state(1)
-        quantise_zs(1)
-        for pair in range(PAIRS):
-            quantise_rows(
-                s_sb[:, blocks_of(pair), :],
-                s_grouped[:, pair],
-                s_codes[:, columns_of(pair)],
-                s_scales[:, columns_of(pair)],
+            load_xg(0, 0)
+            nc.sync.dma_start(out=bias_row[0:1, :], in_=b_gate.unsqueeze(0))
+            nc.sync.dma_start(
+                out=w_sb[:].rearrange("p (u e) n -> p u (e n)", u=HALVES),
+                in_=W_gate.rearrange("(u p e) n -> p u (e n)", u=HALVES, e=2),
             )
-        hop_of_x()
-        hop_of_zs(0)
-        r_of(1)
-        hop_of_zs(1)
+            load_xg(0, 1)
+            load_xg(1, 0)
+            load_xg(1, 1)
+            nc.sync.dma_start(out=x_sb[:], in_=x.rearrange("b (p j) c -> p b j c", j=PACK))
+            nc.sync.dma_start(out=s_sb[:], in_=rows_of(supports))
+            nc.sync.dma_start(out=state_sb[:], in_=state.rearrange("b (p j) c -> p b j c", j=PACK))
+
+            turn_xg(0, 0, 1)
+            bias_ps = psum.tile([P, H + 1], F32, tag="bank")
+            nc.tensor.matmul(out=bias_ps[:, 0:H], lhsT=ones[:], rhs=bias_row[:, H:G], start=True, stop=True)
+            nc.tensor.matmul(
+                out=bias_ps[:, H : H + 1], lhsT=bias_row[:, 0:H], rhs=ones[:, 0:1], start=True, stop=True
+            )
+            nc.scalar.copy(out=bias[:], in_=bias_ps[:])
+            nc.vector.tensor_copy(out=w_grouped[:], in_=w_sb[:].rearrange("p t c -> p c t"))
+            quantise_xg(0, 0)
+            quantise(w_grouped[:].rearrange("p c t -> p (c t)"), w_codes[:], w_scales[:])
+            turn_xg(0, 2, 3)
+            quantise_xg(0, 1)
+            turn_xg(1, 0, 1)
+            nc.vector.tensor_copy(out=cand[:, :, :, 0:H], in_=x_sb[:])
+            for b in range(B):
+                nc.sync.dma_start(out=rows_of(out_1[b])[:, :, 0:H], in_=cand[:, b, :, 0:H])
+            quantise_xg(1, 0)
+            turn_xg(1, 2, 3)
+            quantise_xg(1, 1)
+            z_of(0)
+            nc.vector.tensor_copy(out=x_grouped[:], in_=x_sb[:].rearrange("p b t c -> p b c t"))
+            r_sums(0)
+            turn_s(0)
+            z_of(1)
+            quantise(x_grouped[:].rearrange("p b c t -> p (b c t)"), x_codes[:], x_scales[:])
+            r_of(0)
+            r_sums(1)
+            z_times_state(0)
+            z_times_state(1)
+            r_of(1)
+            turn_s(1)
+            round_zs(0, nc.scalar.copy)
+            quantise_s(0)
+            round_zs(1, nc.vector.tensor_copy)
+            turn_s(2, 3)
+            quantise_zs(0)
+            quantise_zs(1)
+            quantise_s(1)
+            hop_of_x(0, nc.scalar.copy)
+            hop_of_zs(0, 0, nc.vector.tensor_copy)
+            hop_of_zs(1, 0, nc.scalar.copy)
+            store_c1(0)
+            hop_of_x(1, nc.vector.tensor_copy)
+            hop_of_zs(0, 1, nc.scalar.copy)
+            hop_of_zs(1, 1, nc.scalar.copy)
+            store_c1(1)

@@ -92,6 +92,12 @@ def tile_agcrncell_pb_s_kernel(
             for j in blocks:
                 collect(turn(s_sb[:, j, :], "r (p u) -> r u p"), s_grouped[:, j])
 
+        def interleave(copy, grouped, rows):
+            copy(
+                out=grouped.rearrange("p (c i) t -> p c t i", i=4),
+                in_=rows.rearrange("p t (c i) -> p c t i", i=4),
+            )
+
         def quantise(grouped, codes, scales):
             nc.vector.quantize_mx(out=codes.bitcast(FP8X4), scales=scales, in_=grouped)
 
@@ -142,7 +148,7 @@ def tile_agcrncell_pb_s_kernel(
             nc.sync.dma_start(out=rows_of(out_1[b])[:, :, H:G], in_=cand[:, b, :, H:G])
 
         def round_zs(b, copy):
-            copy(out=zs_grouped[:, b], in_=cand[:, b, :, H:G].rearrange("p t c -> p c t"))
+            interleave(copy, zs_grouped[:, b], cand[:, b, :, H:G])
 
         def quantise_zs(b):
             quantise(zs_grouped[:, b].rearrange("p c t -> p (c t)"), zs_codes[:, b], zs_scales[:, b])
@@ -194,7 +200,7 @@ def tile_agcrncell_pb_s_kernel(
                 out=bias_ps[:, H : H + 1], lhsT=bias_row[:, 0:H], rhs=ones[:, 0:1], start=True, stop=True
             )
             nc.scalar.copy(out=bias[:], in_=bias_ps[:])
-            nc.vector.tensor_copy(out=w_grouped[:], in_=w_sb[:].rearrange("p t c -> p c t"))
+            interleave(nc.vector.tensor_copy, w_grouped[:], w_sb[:])
             quantise_xg(0, 0)
             quantise(w_grouped[:].rearrange("p c t -> p (c t)"), w_codes[:], w_scales[:])
             turn_xg(0, 2, 3)
@@ -207,7 +213,8 @@ def tile_agcrncell_pb_s_kernel(
             turn_xg(1, 2, 3)
             quantise_xg(1, 1)
             z_of(0)
-            nc.vector.tensor_copy(out=x_grouped[:], in_=x_sb[:].rearrange("p b t c -> p b c t"))
+            for b in range(B):
+                interleave(nc.vector.tensor_copy, x_grouped[:, b], x_sb[:, b])
             r_sums(0)
             turn_s(0)
             z_of(1)

import concourse.mybir as mybir
from concourse.masks import make_identity

BF16 = mybir.dt.bfloat16
F32 = mybir.dt.float32
U32 = mybir.dt.uint32
U8 = mybir.dt.uint8
FP8X4 = mybir.dt.float8_e4m3fn_x4
ADD = mybir.AluOpType.add
MULT = mybir.AluOpType.mult
SIGMOID = mybir.ActivationFunctionType.Sigmoid

P = 128
PACK = 4
B = 2
K = 512
H = 128
G = 2 * H
Z = 0
PAIR = 2
HALVES = 2
BANKS = 8

FLOPS = 2 * (B * K) * K * G + 2 * B * K * K * G


def tile_agcrncell_pb_s_kernel(
    tc, xg, W_gate, b_gate, x, state, supports, out_0, out_1, out_2
):
    nc = tc.nc
    with tc.tile_pool(name="keep", bufs=1) as keep, tc.psum_pool(name="psum", bufs=BANKS) as psum:
        xg_sb = keep.tile([P, B, PACK, K], BF16)
        w_sb = keep.tile([P, PACK, G], BF16)
        s_sb = keep.tile([P, PACK, K], BF16)
        x_sb = keep.tile([P, B, PACK, H], BF16)
        state_sb = keep.tile([P, B, PACK, H], BF16)
        bias_row = keep.tile([P, G], BF16)
        ident = keep.tile([P, P], F32)
        ones = keep.tile([P, P], BF16)
        warm_in = keep.tile([P, 1], F32)
        warm_out = keep.tile([P, 1], F32)
        bias = keep.tile([P, H + 1], F32)

        w_grouped = keep.tile([P, G, PACK], BF16, align_bytes=64)
        w_codes = keep.tile([P, G], U32, align_bytes=64)
        w_scales = keep.tile([P, G], U8, align_bytes=64)
        xg_grouped = keep.tile([P, B, PACK, P, PACK], BF16, align_bytes=64)
        xg_codes = keep.tile([P, B, PACK * P], U32, align_bytes=64)
        xg_scales = keep.tile([P, B, PACK * P], U8, align_bytes=64)
        s_grouped = keep.tile([P, PACK, P, PACK], BF16, align_bytes=64)
        s_codes = keep.tile([P, PACK * P], U32, align_bytes=64)
        s_scales = keep.tile([P, PACK * P], U8, align_bytes=64)
        x_grouped = keep.tile([P, B, H, PACK], BF16, align_bytes=64)
        x_codes = keep.tile([P, B * H], U32, align_bytes=64)
        x_scales = keep.tile([P, B * H], U8, align_bytes=64)
        zs_grouped = keep.tile([P, B, H, PACK], BF16, align_bytes=64)
        zs_codes = keep.tile([P, B, H], U32, align_bytes=64)
        zs_scales = keep.tile([P, B, H], U8, align_bytes=64)

        r_pre = keep.tile([P, B, PACK, H], F32)
        r = keep.tile([P, B, PACK, H], F32)
        z_cols = keep.tile([P, B, PACK, P], F32)
        cand = keep.tile([P, B, PACK, G], F32)
        c1 = keep.tile([P, B, PACK, G], F32)

        def rows_of(dram):
            return dram.rearrange("(p j) n -> p j n", j=PACK)

        def pair_of(h):
            return slice(PAIR * h, PAIR * (h + 1))

        def columns_of(first, count):
            return slice(P * first, P * (first + count))

        make_identity(nc, ident[:])

        def turn(rows, word_order):
            bank = psum.tile([P, HALVES, P], F32, tag="bank")
            words = rows.bitcast(F32).rearrange(word_order, u=HALVES)
            for u in range(HALVES):
                nc.tensor.transpose(bank[:, u, :], words[:, u, :], ident[:])
            return bank

        def collect(bank, grouped):
            nc.scalar.copy(out=grouped.bitcast(F32), in_=bank[:].rearrange("p u r -> p r u"))

        def turn_xg(b, *blocks):
            for j in blocks:
                collect(turn(xg_sb[:, b, j, :], "r (u p) -> r u p"), xg_grouped[:, b, j])

        def turn_s(*blocks):
            for j in blocks:
                collect(turn(s_sb[:, j, :], "r (p u) -> r u p"), s_grouped[:, j])

        def interleave(copy, grouped, rows):
            copy(
                out=grouped.rearrange("p (c i) t -> p c t i", i=4),
                in_=rows.rearrange("p t (c i) -> p c t i", i=4),
            )

        def quantise(grouped, codes, scales):
            nc.vector.quantize_mx(out=codes.bitcast(FP8X4), scales=scales, in_=grouped)

        def quantise_pair(h, grouped, codes, scales):
            cols = columns_of(PAIR * h, PAIR)
            quantise(grouped[:, pair_of(h)].rearrange("p j r t -> p (j r t)"), codes[:, cols], scales[:, cols])

        def quantise_xg(b, h):
            quantise_pair(h, xg_grouped[:, b], xg_codes[:, b], xg_scales[:, b])

        def quantise_s(h):
            quantise_pair(h, s_grouped, s_codes, s_scales)

        def product(out, rows_codes, rows_scales, block, rhs_codes, rhs_scales):
            cols = columns_of(block, 1)
            nc.tensor.matmul_mx(
                out=out,
                lhsT=rows_codes[:, cols].bitcast(FP8X4),
                lhsT_scale=rows_scales[:, cols],
                rhs=rhs_codes.bitcast(FP8X4),
                rhs_scale=rhs_scales,
                start=True,
                stop=True,
            )

        def z_of(b):
            acc = psum.tile([P, PACK, P], F32, tag="bank")
            product(acc[:].rearrange("c j i -> c (j i)"), w_codes, w_scales, Z, xg_codes[:, b], xg_scales[:, b])
            nc.scalar.activation(out=z_cols[:, b], in_=acc[:], func=SIGMOID, bias=bias[:, H : H + 1])

        def r_sums(b):
            acc = psum.tile([P, PACK, H], F32, tag="bank")
            for j in range(PACK):
                product(acc[:, j, :], xg_codes[:, b], xg_scales[:, b], j, w_codes[:, H:G], w_scales[:, H:G])
            nc.vector.tensor_tensor(
                out=r_pre[:, b], in0=acc[:], in1=bias[:, 0:H].unsqueeze(1).to_broadcast([P, PACK, H]), op=ADD
            )

        def r_of(b):
            nc.scalar.activation(out=r[:, b], in_=r_pre[:, b], func=SIGMOID)
            nc.sync.dma_start(out=rows_of(out_0[b]), in_=r[:, b])

        def z_times_state(b):
            z_rows = psum.tile([P, PACK, H], F32, tag="bank")
            for j in range(PACK):
                nc.tensor.transpose(z_rows[:, j, :], z_cols[:, b, j, :], ident[:])
            nc.vector.tensor_tensor(out=cand[:, b, :, H:G], in0=z_rows[:], in1=state_sb[:, b], op=MULT)
            nc.sync.dma_start(out=rows_of(out_1[b])[:, :, H:G], in_=cand[:, b, :, H:G])

        def round_zs(b, copy):
            interleave(copy, zs_grouped[:, b], cand[:, b, :, H:G])

        def quantise_zs(b):
            quantise(zs_grouped[:, b].rearrange("p c t -> p (c t)"), zs_codes[:, b], zs_scales[:, b])

        def hop_of_x(h, copy):
            hop = psum.tile([P, PAIR, B, H], F32, tag="bank")
            for i in range(PAIR):
                product(
                    hop[:, i].rearrange("p b c -> p (b c)"), s_codes, s_scales, PAIR * h + i, x_codes[:], x_scales[:]
                )
            copy(out=c1[:, :, pair_of(h), 0:H], in_=hop[:].rearrange("p i b c -> p b i c"))

        def hop_of_zs(b, h, copy):
            hop = psum.tile([P, PAIR, H], F32, tag="bank")
            for i in range(PAIR):
                product(hop[:, i, :], s_codes, s_scales, PAIR * h + i, zs_codes[:, b], zs_scales[:, b])
            copy(out=c1[:, b, pair_of(h), H:G], in_=hop[:])

        def store_c1(h):
            for b in range(B):
                nc.sync.dma_start(out=rows_of(out_2[b])[:, pair_of(h), :], in_=c1[:, b, pair_of(h), :])

        def load_xg(b, h):
            nc.sync.dma_start(out=xg_sb[:, b, pair_of(h), :], in_=rows_of(xg[b])[:, pair_of(h), :])

        with tc.manual_schedule():
            nc.vector.memset(warm_in[:], 0.0)
            nc.vector.memset(bias_row[:], 0.0)
            nc.vector.memset(ones[:], 1.0)
            nc.scalar.activation(out=warm_out[:], in_=warm_in[:], func=SIGMOID)

            load_xg(0, 0)
            nc.sync.dma_start(out=bias_row[0:1, :], in_=b_gate.unsqueeze(0))
            nc.sync.dma_start(
                out=w_sb[:].rearrange("p (u e) n -> p u (e n)", u=HALVES),
                in_=W_gate.rearrange("(u p e) n -> p u (e n)", u=HALVES, e=2),
            )
            load_xg(0, 1)
            load_xg(1, 0)
            load_xg(1, 1)
            nc.sync.dma_start(out=x_sb[:], in_=x.rearrange("b (p j) c -> p b j c", j=PACK))
            nc.sync.dma_start(out=s_sb[:], in_=rows_of(supports))
            nc.sync.dma_start(out=state_sb[:], in_=state.rearrange("b (p j) c -> p b j c", j=PACK))

            turn_xg(0, 0, 1)
            bias_ps = psum.tile([P, H + 1], F32, tag="bank")
            nc.tensor.matmul(out=bias_ps[:, 0:H], lhsT=ones[:], rhs=bias_row[:, H:G], start=True, stop=True)
            nc.tensor.matmul(
                out=bias_ps[:, H : H + 1], lhsT=bias_row[:, 0:H], rhs=ones[:, 0:1], start=True, stop=True
            )
            nc.scalar.copy(out=bias[:], in_=bias_ps[:])
            interleave(nc.vector.tensor_copy, w_grouped[:], w_sb[:])
            quantise_xg(0, 0)
            quantise(w_grouped[:].rearrange("p c t -> p (c t)"), w_codes[:], w_scales[:])
            turn_xg(0, 2, 3)
            quantise_xg(0, 1)
            turn_xg(1, 0, 1)
            nc.vector.tensor_copy(out=cand[:, :, :, 0:H], in_=x_sb[:])
            for b in range(B):
                nc.sync.dma_start(out=rows_of(out_1[b])[:, :, 0:H], in_=cand[:, b, :, 0:H])
            quantise_xg(1, 0)
            turn_xg(1, 2, 3)
            quantise_xg(1, 1)
            z_of(0)
            for b in range(B):
                interleave(nc.vector.tensor_copy, x_grouped[:, b], x_sb[:, b])
            r_sums(0)
            turn_s(0)
            z_of(1)
            quantise(x_grouped[:].rearrange("p b c t -> p (b c t)"), x_codes[:], x_scales[:])
            r_of(0)
            r_sums(1)
            z_times_state(0)
            z_times_state(1)
            r_of(1)
            turn_s(1)
            round_zs(0, nc.scalar.copy)
            quantise_s(0)
            round_zs(1, nc.vector.tensor_copy)
            turn_s(2, 3)
            quantise_zs(0)
            quantise_zs(1)
            quantise_s(1)
            hop_of_x(0, nc.scalar.copy)
            hop_of_zs(0, 0, nc.vector.tensor_copy)
            hop_of_zs(1, 0, nc.scalar.copy)
            store_c1(0)
            hop_of_x(1, nc.vector.tensor_copy)
            hop_of_zs(0, 1, nc.scalar.copy)
            hop_of_zs(1, 1, nc.scalar.copy)
            store_c1(1)
